import numpy as np
import ml_dtypes


def mxq(x, axis, fmt="e4m3"):
    dtype, down = {"e4m3": (ml_dtypes.float8_e4m3fn, 7), "e5m2": (ml_dtypes.float8_e5m2, 14)}[fmt]
    v = np.moveaxis(np.asarray(x, np.float32).astype(ml_dtypes.bfloat16).astype(np.float64), axis, -1)
    blocks = v.reshape(v.shape[:-1] + (-1, 32))
    amax = np.abs(blocks).max(-1, keepdims=True)
    byte = np.maximum(np.where(amax > 0, np.frexp(amax)[1] - 1 + 127, 0) - down, 1)
    scale = np.exp2(byte - 127.0)
    codes = (blocks / scale).astype(np.float32).astype(dtype).astype(np.float64)
    return np.moveaxis((codes * scale).reshape(v.shape), -1, axis)


WIDE = False


def mx_kscale(k):
    if not WIDE:
        return np.ones(k)
    levels = np.array([10, -10, 5, -5, 0])
    if k % 512:
        return np.exp2(np.random.permutation(np.resize(levels, k // 32))).repeat(32)
    a = np.empty((k // 512, 16))
    for p in range(k // 512):
        a[p, :8] = np.random.permutation(np.resize(levels, 8))
        for g in range(8):
            far = levels[np.abs(levels - a[p, g]) >= 10]
            a[p, g + 8] = far[np.random.randint(len(far))]
    return np.exp2(a.ravel()).repeat(32)


BF16 = ml_dtypes.bfloat16


def bf(x):
    return np.asarray(x, np.float32).astype(BF16)


def f64(x):
    return np.asarray(x).astype(np.float64)


B, S, H, NH, FF = 2, 512, 1024, 8, 3072
EPS = 1e-7


def layer_norm(x, g, b):
    m = x.mean(-1, keepdims=True)
    v = ((x - m) ** 2).mean(-1, keepdims=True)
    return (x - m) / np.sqrt(v + EPS) * g + b


def setup_inputs():
    s = mx_kscale(FF)
    r = np.random.standard_normal
    return {"ff": bf(r((B, S, FF)) * 0.65 * s), "attn_out": bf(r((B, S, H))),
            "Wf": bf(r((FF, H)) * 1.5 / np.sqrt(FF) / s[:, None]), "b_f": bf(r(H) * 0.2),
            "ln2_g": bf(1.0 + 0.1 * r(H)), "ln2_b": bf(0.1 * r(H))}


def reference(ff, attn_out, Wf, b_f, ln2_g, ln2_b):
    u = (mxq(f64(ff), 2, "e4m3") @ mxq(f64(Wf), 0, "e4m3")) + f64(b_f) + f64(attn_out)
    return layer_norm(u, f64(ln2_g), f64(ln2_b))

@@ -1,0 +1,276 @@
+from contextlib import ExitStack
+
+import concourse.mybir as mybir
+from concourse.masks import make_identity
+
+F32 = mybir.dt.float32
+BF16 = mybir.dt.bfloat16
+U32 = mybir.dt.uint32
+U8 = mybir.dt.uint8
+FP8X4 = mybir.dt.float8_e4m3fn_x4
+ALU = mybir.AluOpType
+ACT = mybir.ActivationFunctionType
+
+P = 128
+PACK = 4
+K_PASS = P * PACK
+TOKENS = 1024
+K = 3072
+N = 1024
+EPS = 1e-7
+PASSES = K // K_PASS
+TILES = TOKENS // P
+BANK = 512
+HALVES = N // BANK
+FILLS = K // 2 // BANK
+PASSES_PER_FILL = PASSES // FILLS
+
+EARLY_TILES = 2
+STAGE_BANKS = 8 - EARLY_TILES * HALVES
+W_VECTOR_COLS = 512
+
+FLOPS = 2 * TOKENS * K * N
+
+
+def tile_disentangledattention_pc_kernel(tc, ff, attn_out, Wf, b_f, ln2_g, ln2_b, out):
+    nc = tc.nc
+    ff_rows = ff.flatten_outer_dims()
+    attn_rows = attn_out.flatten_outer_dims()
+    out_rows = out.flatten_outer_dims()
+
+    with ExitStack() as ctx:
+        const = ctx.enter_context(tc.tile_pool(name="const", bufs=1))
+        ff_pool = ctx.enter_context(tc.tile_pool(name="ff", bufs=TILES))
+        attn_pool = ctx.enter_context(tc.tile_pool(name="attn", bufs=TILES))
+        w_raw_pool = ctx.enter_context(tc.tile_pool(name="w_raw", bufs=4))
+        w_grouped_pool = ctx.enter_context(tc.tile_pool(name="w_grouped", bufs=2))
+        x_grouped_pool = ctx.enter_context(tc.tile_pool(name="x_grouped", bufs=2))
+        x_pool = ctx.enter_context(tc.tile_pool(name="x", bufs=EARLY_TILES + 2))
+        resid_pool = ctx.enter_context(tc.tile_pool(name="resid", bufs=3))
+        u_pool = ctx.enter_context(tc.tile_pool(name="u", bufs=2))
+        y_pool = ctx.enter_context(tc.tile_pool(name="y", bufs=3))
+        scratch = ctx.enter_context(tc.tile_pool(name="scratch", bufs=2))
+        stats = ctx.enter_context(tc.tile_pool(name="stats", bufs=4))
+        acc_pool = ctx.enter_context(tc.psum_pool(name="acc", bufs=EARLY_TILES * HALVES))
+        stage = ctx.enter_context(tc.psum_pool(name="stage", bufs=STAGE_BANKS))
+
+        ident_words = const.tile([P, P], F32)
+        make_identity(nc, ident_words[:])
+        ident_bf16 = const.tile([P, P], BF16)
+        make_identity(nc, ident_bf16[:])
+        vector_rows = const.tile([P, N], BF16)
+        nc.vector.memset(vector_rows[:], 0.0)
+        pick = const.tile([P, 3, P], BF16)
+        nc.vector.memset(pick[:], 0.0)
+        for j, vec in enumerate((b_f, ln2_g, ln2_b)):
+            nc.sync.dma_start(out=vector_rows[32 * j : 32 * j + 1, :], in_=vec.rearrange("(o n) -> o n", o=1))
+            nc.vector.memset(pick[32 * j : 32 * j + 1, j, :], 1.0)
+        eps = const.tile([P, 1], F32)
+        nc.vector.memset(eps[:], EPS)
+        warm = const.tile([P, 1], F32)
+        nc.scalar.activation(out=warm[:], in_=eps[:], func=ACT.Sqrt)
+        gamma = const.tile([P, N], F32)
+        beta = const.tile([P, N], F32)
+
+        def spread_gain_and_shift():
+            for h in range(HALVES):
+                cols = slice(h * BANK, (h + 1) * BANK)
+                gamma_bank = stage.tile([P, BANK], F32, name="bank")
+                nc.tensor.matmul(out=gamma_bank[:], lhsT=pick[:, 1, :], rhs=vector_rows[:, cols], start=True, stop=True)
+                nc.vector.tensor_copy(out=gamma[:, cols], in_=gamma_bank[:])
+                beta_bank = stage.tile([P, BANK], F32, name="bank")
+                nc.tensor.matmul(out=beta_bank[:], lhsT=pick[:, 2, :], rhs=vector_rows[:, cols], start=True, stop=True)
+                nc.scalar.copy(out=beta[:, cols], in_=beta_bank[:])
+
+        w_codes = const.tile([P, PASSES, N], U32, align_bytes=64)
+        w_scales = const.tile([P, PASSES, N], U8, align_bytes=64)
+
+        ff_tile, attn_tile, w_raw, w_grouped = {}, {}, {}, {}
+        x_grouped, x_codes, x_scales = {}, {}, {}
+        acc, resid, u, y, neg_mean, std = {}, {}, {}, {}, {}, {}
+
+        def load_tokens(m):
+            ff_tile[m] = ff_pool.tile([P, K], BF16, name="ff_tile")
+            nc.sync.dma_start(out=ff_tile[m][:], in_=ff_rows[m * P : (m + 1) * P, :])
+
+        def load_residual(m):
+            attn_tile[m] = attn_pool.tile([P, N], BF16, name="attn_tile")
+            nc.sync.dma_start(out=attn_tile[m][:], in_=attn_rows[m * P : (m + 1) * P, :])
+
+        def load_weights(g):
+            w_raw[g] = w_raw_pool.tile([P, PACK, N], BF16, name="w_raw")
+            nc.sync.dma_start(
+                out=w_raw[g][:], in_=Wf[g * K_PASS : (g + 1) * K_PASS, :].rearrange("(p t) c -> p t c", t=PACK)
+            )
+
+        def regroup_weights(g):
+            w_grouped[g] = w_grouped_pool.tile([P, N, PACK], BF16, name="w_grouped", align_bytes=64)
+            left = slice(0, W_VECTOR_COLS)
+            right = slice(W_VECTOR_COLS, N)
+            nc.vector.tensor_copy(
+                out=w_grouped[g][:, left, :].rearrange("p (c i) t -> p c t i", i=4),
+                in_=w_raw[g][:, :, left].rearrange("p t (c i) -> p c t i", i=4),
+            )
+            nc.scalar.copy(
+                out=w_grouped[g][:, right, :].rearrange("p (c i) t -> p c t i", i=4),
+                in_=w_raw[g][:, :, right].rearrange("p t (c i) -> p c t i", i=4),
+            )
+
+        def quantise_weights(g):
+            for h in range(HALVES):
+                cols = slice(h * BANK, (h + 1) * BANK)
+                nc.vector.quantize_mx(
+                    out=w_codes[:, g, cols].bitcast(FP8X4),
+                    scales=w_scales[:, g, cols],
+                    in_=w_grouped[g][:, cols, :].rearrange("p c t -> p (c t)"),
+                )
+
+        def transpose_tokens(m, j):
+            if j == 0:
+                x_grouped[m] = x_grouped_pool.tile([P, PASSES * P * PACK], BF16, name="x_grouped", align_bytes=64)
+            words = ff_tile[m][:].bitcast(F32)
+            bank = stage.tile([P, BANK], F32, name="bank")
+            for q in range(BANK // P):
+                g, u = divmod(q, 2)
+                first = j * BANK + g * 2 * P
+                nc.tensor.transpose(
+                    bank[:, q * P : (q + 1) * P], words[:, first + u : first + 2 * P : 2], ident_words[:]
+                )
+            nc.scalar.copy(
+                out=x_grouped[m][:].bitcast(F32)[:, j * BANK : (j + 1) * BANK].rearrange(
+                    "p (g r u) -> p g r u", g=PASSES_PER_FILL, u=2
+                ),
+                in_=bank[:].rearrange("p (g u r) -> p g r u", g=PASSES_PER_FILL, u=2),
+            )
+
+        def quantise_tokens(m):
+            x_codes[m] = x_pool.tile([P, PASSES * P], U32, name="x_codes", align_bytes=64)
+            x_scales[m] = x_pool.tile([P, PASSES * P], U8, name="x_scales", align_bytes=64)
+            width = PASSES_PER_FILL * P
+            for j in range(FILLS):
+                nc.vector.quantize_mx(
+                    out=x_codes[m][:, j * width : (j + 1) * width].bitcast(FP8X4),
+                    scales=x_scales[m][:, j * width : (j + 1) * width],
+                    in_=x_grouped[m][:, j * width * PACK : (j + 1) * width * PACK],
+                )
+
+        def multiply(m, g):
+            if g == 0:
+                acc[m] = [acc_pool.tile([P, BANK], F32, name="acc") for h in range(HALVES)]
+            tokens = slice(g * P, (g + 1) * P)
+            for h in range(HALVES):
+                cols = slice(h * BANK, (h + 1) * BANK)
+                nc.tensor.matmul_mx(
+                    out=acc[m][h][:],
+                    lhsT=x_codes[m][:, tokens].bitcast(FP8X4),
+                    lhsT_scale=x_scales[m][:, tokens],
+                    rhs=w_codes[:, g, cols].bitcast(FP8X4),
+                    rhs_scale=w_scales[:, g, cols],
+                    start=(g == 0),
+                    stop=(g == PASSES - 1),
+                )
+
+        def add_residual_and_bias(m):
+            resid[m] = resid_pool.tile([P, N], F32, name="resid")
+            for h in range(HALVES):
+                cols = slice(h * BANK, (h + 1) * BANK)
+                bank = stage.tile([P, BANK], F32, name="bank")
+                nc.tensor.matmul(out=bank[:], lhsT=ident_bf16[:], rhs=attn_tile[m][:, cols], start=True, stop=False)
+                nc.tensor.matmul(out=bank[:], lhsT=pick[:, 0, :], rhs=vector_rows[:, cols], start=False, stop=True)
+                nc.scalar.copy(out=resid[m][:, cols], in_=bank[:])
+
+        def form_u(m):
+            u[m] = u_pool.tile([P, N], F32, name="u")
+            half_sums = stats.tile([P, HALVES], F32, name="half_sums")
+            for h in range(HALVES):
+                cols = slice(h * BANK, (h + 1) * BANK)
+                nc.vector.scalar_tensor_tensor(
+                    out=u[m][:, cols],
+                    in0=acc[m][h][:],
+                    scalar=1.0,
+                    in1=resid[m][:, cols],
+                    op0=ALU.mult,
+                    op1=ALU.add,
+                    accum_out=half_sums[:, h : h + 1],
+                )
+            neg_mean[m] = stats.tile([P, 1], F32, name="neg_mean")
+            nc.vector.tensor_scalar(
+                out=neg_mean[m][:],
+                in0=half_sums[:, 0:1],
+                scalar1=half_sums[:, 1:2],
+                scalar2=-1.0 / N,
+                op0=ALU.add,
+                op1=ALU.mult,
+            )
+
+        def deviation(m):
+            squares = scratch.tile([P, N], BF16, name="squares")
+            sum_squares = stats.tile([P, 1], F32, name="sum_squares")
+            nc.scalar.activation(
+                out=squares[:], in_=u[m][:], func=ACT.Square, bias=neg_mean[m][:], scale=1.0, accum_out=sum_squares[:]
+            )
+            std[m] = stats.tile([P, 1], F32, name="std")
+            nc.scalar.activation(out=std[m][:], in_=sum_squares[:], func=ACT.Sqrt, bias=eps[:], scale=1.0 / N)
+
+        def centre_and_gain(m):
+            y[m] = y_pool.tile([P, N], F32, name="y")
+            nc.vector.scalar_tensor_tensor(
+                out=y[m][:], in0=u[m][:], scalar=neg_mean[m][:], in1=gamma[:], op0=ALU.add, op1=ALU.mult
+            )
+
+        def scale_shift_store(m):
+            rstd = stats.tile([P, 1], F32, name="rstd")
+            nc.vector.reciprocal(out=rstd[:], in_=std[m][:])
+            nc.vector.scalar_tensor_tensor(
+                out=y[m][:], in0=y[m][:], scalar=rstd[:], in1=beta[:], op0=ALU.mult, op1=ALU.add
+            )
+            nc.sync.dma_start(out=out_rows[m * P : (m + 1) * P, :], in_=y[m][:])
+
+        for step in range(PASSES):
+            load_weights(step)
+            if step < EARLY_TILES:
+                load_tokens(step)
+            if step == 0:
+                spread_gain_and_shift()
+            regroup_weights(step)
+            if 1 <= step <= EARLY_TILES:
+                quantise_tokens(step - 1)
+            quantise_weights(step)
+            if step < EARLY_TILES:
+                for j in range(FILLS):
+                    transpose_tokens(step, j)
+            if step == PASSES - 1:
+                load_residual(0)
+                add_residual_and_bias(0)
+            for m in range(EARLY_TILES):
+                for g in range(PASSES):
+                    if max(m + 1, g) == step:
+                        multiply(m, g)
+
+        for m in range(EARLY_TILES, TILES):
+            load_tokens(m)
+            load_residual(m - EARLY_TILES + 1)
+        for m in range(TILES - EARLY_TILES + 1, TILES):
+            load_residual(m)
+        for j in range(FILLS):
+            transpose_tokens(EARLY_TILES, j)
+
+        for s in range(TILES):
+            multiplied = s + EARLY_TILES
+            transposed = multiplied + 1
+            if s + 1 < TILES:
+                add_residual_and_bias(s + 1)
+            form_u(s)
+            deviation(s)
+            if s >= 1:
+                scale_shift_store(s - 1)
+            centre_and_gain(s)
+            if multiplied < TILES:
+                quantise_tokens(multiplied)
+            if transposed < TILES:
+                for j in range(FILLS):
+                    transpose_tokens(transposed, j)
+            if multiplied < TILES:
+                for g in range(PASSES):
+                    multiply(multiplied, g)
+        scale_shift_store(TILES - 1)

@@ -25,9 +25,10 @@ HALVES = N // BANK
 FILLS = K // 2 // BANK
 PASSES_PER_FILL = PASSES // FILLS
 
-EARLY_TILES = 2
-STAGE_BANKS = 8 - EARLY_TILES * HALVES
-W_VECTOR_COLS = 512
+EARLY_TILES = 3
+ACC_BANKS = 4
+STAGE_BANKS = 8 - ACC_BANKS
+W_VECTOR_COLS = 352
 
 FLOPS = 2 * TOKENS * K * N
 
@@ -42,52 +43,59 @@ def tile_disentangledattention_pc_kernel(tc, ff, attn_out, Wf, b_f, ln2_g, ln2_b
         const = ctx.enter_context(tc.tile_pool(name="const", bufs=1))
         ff_pool = ctx.enter_context(tc.tile_pool(name="ff", bufs=TILES))
         attn_pool = ctx.enter_context(tc.tile_pool(name="attn", bufs=TILES))
-        w_raw_pool = ctx.enter_context(tc.tile_pool(name="w_raw", bufs=4))
-        w_grouped_pool = ctx.enter_context(tc.tile_pool(name="w_grouped", bufs=2))
+        w_raw_pool = ctx.enter_context(tc.tile_pool(name="w_raw", bufs=6))
+        w_grouped_pool = ctx.enter_context(tc.tile_pool(name="w_grouped", bufs=3))
         x_grouped_pool = ctx.enter_context(tc.tile_pool(name="x_grouped", bufs=2))
-        x_pool = ctx.enter_context(tc.tile_pool(name="x", bufs=EARLY_TILES + 2))
-        resid_pool = ctx.enter_context(tc.tile_pool(name="resid", bufs=3))
-        u_pool = ctx.enter_context(tc.tile_pool(name="u", bufs=2))
+        x_pool = ctx.enter_context(tc.tile_pool(name="x", bufs=EARLY_TILES + 3))
+        resid_pool = ctx.enter_context(tc.tile_pool(name="resid", bufs=6))
+        u_pool = ctx.enter_context(tc.tile_pool(name="u", bufs=EARLY_TILES + 2))
         y_pool = ctx.enter_context(tc.tile_pool(name="y", bufs=3))
         scratch = ctx.enter_context(tc.tile_pool(name="scratch", bufs=2))
-        stats = ctx.enter_context(tc.tile_pool(name="stats", bufs=4))
-        acc_pool = ctx.enter_context(tc.psum_pool(name="acc", bufs=EARLY_TILES * HALVES))
+        stats = ctx.enter_context(tc.tile_pool(name="stats", bufs=TILES))
+        acc_pool = ctx.enter_context(tc.psum_pool(name="acc", bufs=ACC_BANKS))
         stage = ctx.enter_context(tc.psum_pool(name="stage", bufs=STAGE_BANKS))
+        ctx.enter_context(tc.manual_schedule())
 
         ident_words = const.tile([P, P], F32)
         make_identity(nc, ident_words[:])
         ident_bf16 = const.tile([P, P], BF16)
         make_identity(nc, ident_bf16[:])
-        vector_rows = const.tile([P, N], BF16)
-        nc.vector.memset(vector_rows[:], 0.0)
-        pick = const.tile([P, 3, P], BF16)
-        nc.vector.memset(pick[:], 0.0)
-        for j, vec in enumerate((b_f, ln2_g, ln2_b)):
-            nc.sync.dma_start(out=vector_rows[32 * j : 32 * j + 1, :], in_=vec.rearrange("(o n) -> o n", o=1))
-            nc.vector.memset(pick[32 * j : 32 * j + 1, j, :], 1.0)
         eps = const.tile([P, 1], F32)
         nc.vector.memset(eps[:], EPS)
-        warm = const.tile([P, 1], F32)
-        nc.scalar.activation(out=warm[:], in_=eps[:], func=ACT.Sqrt)
+        vector_rows = const.tile([P, N], BF16)
+        nc.vector.memset(vector_rows[:].bitcast(U32), 0)
+        pick = const.tile([P, 3, P], BF16)
+        nc.vector.memset(pick[:].rearrange("p j m -> p (j m)").bitcast(U32), 0)
+        for j in range(3):
+            nc.vector.memset(pick[32 * j : 32 * j + 1, j, :], 1.0)
         gamma = const.tile([P, N], F32)
         beta = const.tile([P, N], F32)
 
-        def spread_gain_and_shift():
-            for h in range(HALVES):
-                cols = slice(h * BANK, (h + 1) * BANK)
-                gamma_bank = stage.tile([P, BANK], F32, name="bank")
-                nc.tensor.matmul(out=gamma_bank[:], lhsT=pick[:, 1, :], rhs=vector_rows[:, cols], start=True, stop=True)
-                nc.vector.tensor_copy(out=gamma[:, cols], in_=gamma_bank[:])
-                beta_bank = stage.tile([P, BANK], F32, name="bank")
-                nc.tensor.matmul(out=beta_bank[:], lhsT=pick[:, 2, :], rhs=vector_rows[:, cols], start=True, stop=True)
-                nc.scalar.copy(out=beta[:, cols], in_=beta_bank[:])
+        warm = const.tile([P, 1], F32)
+        nc.scalar.activation(out=warm[:], in_=eps[:], func=ACT.Abs_reciprocal_sqrt)
+
+        def load_vectors():
+            for j, vec in enumerate((b_f, ln2_g, ln2_b)):
+                nc.sync.dma_start(out=vector_rows[32 * j : 32 * j + 1, :], in_=vec.rearrange("(o n) -> o n", o=1))
+
+        def spread_gain_and_shift(h):
+            cols = slice(h * BANK, (h + 1) * BANK)
+            gamma_bank = stage.tile([P, BANK], F32, name="bank")
+            nc.tensor.matmul(out=gamma_bank[:], lhsT=pick[:, 1, :], rhs=vector_rows[:, cols], start=True, stop=True)
+            nc.vector.tensor_copy(out=gamma[:, cols], in_=gamma_bank[:])
+            beta_bank = stage.tile([P, BANK], F32, name="bank")
+            nc.tensor.matmul(out=beta_bank[:], lhsT=pick[:, 2, :], rhs=vector_rows[:, cols], start=True, stop=True)
+            nc.scalar.copy(out=beta[:, cols], in_=beta_bank[:])
 
         w_codes = const.tile([P, PASSES, N], U32, align_bytes=64)
         w_scales = const.tile([P, PASSES, N], U8, align_bytes=64)
 
         ff_tile, attn_tile, w_raw, w_grouped = {}, {}, {}, {}
         x_grouped, x_codes, x_scales = {}, {}, {}
-        acc, resid, u, y, neg_mean, std = {}, {}, {}, {}, {}, {}
+        acc, resid, u, y, half_sums, neg_mean, rstd = {}, {}, {}, {}, {}, {}, {}
+
+        def half(h):
+            return slice(h * BANK, (h + 1) * BANK)
 
         def load_tokens(m):
             ff_tile[m] = ff_pool.tile([P, K], BF16, name="ff_tile")
@@ -97,33 +105,32 @@ def tile_disentangledattention_pc_kernel(tc, ff, attn_out, Wf, b_f, ln2_g, ln2_b
             attn_tile[m] = attn_pool.tile([P, N], BF16, name="attn_tile")
             nc.sync.dma_start(out=attn_tile[m][:], in_=attn_rows[m * P : (m + 1) * P, :])
 
-        def load_weights(g):
-            w_raw[g] = w_raw_pool.tile([P, PACK, N], BF16, name="w_raw")
+        def load_weights(g, h):
+            w_raw[g, h] = w_raw_pool.tile([P, PACK, BANK], BF16, name="w_raw")
             nc.sync.dma_start(
-                out=w_raw[g][:], in_=Wf[g * K_PASS : (g + 1) * K_PASS, :].rearrange("(p t) c -> p t c", t=PACK)
+                out=w_raw[g, h][:],
+                in_=Wf[g * K_PASS : (g + 1) * K_PASS, half(h)].rearrange("(p t) c -> p t c", t=PACK),
             )
 
-        def regroup_weights(g):
-            w_grouped[g] = w_grouped_pool.tile([P, N, PACK], BF16, name="w_grouped", align_bytes=64)
+        def regroup_weights(g, h):
+            w_grouped[g, h] = w_grouped_pool.tile([P, BANK, PACK], BF16, name="w_grouped", align_bytes=64)
             left = slice(0, W_VECTOR_COLS)
-            right = slice(W_VECTOR_COLS, N)
-            nc.vector.tensor_copy(
-                out=w_grouped[g][:, left, :].rearrange("p (c i) t -> p c t i", i=4),
-                in_=w_raw[g][:, :, left].rearrange("p t (c i) -> p c t i", i=4),
-            )
+            right = slice(W_VECTOR_COLS, BANK)
             nc.scalar.copy(
-                out=w_grouped[g][:, right, :].rearrange("p (c i) t -> p c t i", i=4),
-                in_=w_raw[g][:, :, right].rearrange("p t (c i) -> p c t i", i=4),
+                out=w_grouped[g, h][:, right, :].rearrange("p (c i) t -> p c t i", i=4),
+                in_=w_raw[g, h][:, :, right].rearrange("p t (c i) -> p c t i", i=4),
+            )
+            nc.vector.tensor_copy(
+                out=w_grouped[g, h][:, left, :].rearrange("p (c i) t -> p c t i", i=4),
+                in_=w_raw[g, h][:, :, left].rearrange("p t (c i) -> p c t i", i=4),
             )
 
-        def quantise_weights(g):
-            for h in range(HALVES):
-                cols = slice(h * BANK, (h + 1) * BANK)
-                nc.vector.quantize_mx(
-                    out=w_codes[:, g, cols].bitcast(FP8X4),
-                    scales=w_scales[:, g, cols],
-                    in_=w_grouped[g][:, cols, :].rearrange("p c t -> p (c t)"),
-                )
+        def quantise_weights(g, h):
+            nc.vector.quantize_mx(
+                out=w_codes[:, g, half(h)].bitcast(FP8X4),
+                scales=w_scales[:, g, half(h)],
+                in_=w_grouped[g, h][:].rearrange("p c t -> p (c t)"),
+            )
 
         def transpose_tokens(m, j):
             if j == 0:
@@ -131,10 +138,10 @@ def tile_disentangledattention_pc_kernel(tc, ff, attn_out, Wf, b_f, ln2_g, ln2_b
             words = ff_tile[m][:].bitcast(F32)
             bank = stage.tile([P, BANK], F32, name="bank")
             for q in range(BANK // P):
-                g, u = divmod(q, 2)
+                g, u_slot = divmod(q, 2)
                 first = j * BANK + g * 2 * P
                 nc.tensor.transpose(
-                    bank[:, q * P : (q + 1) * P], words[:, first + u : first + 2 * P : 2], ident_words[:]
+                    bank[:, q * P : (q + 1) * P], words[:, first + u_slot : first + 2 * P : 2], ident_words[:]
                 )
             nc.scalar.copy(
                 out=x_grouped[m][:].bitcast(F32)[:, j * BANK : (j + 1) * BANK].rearrange(
@@ -154,63 +161,56 @@ def tile_disentangledattention_pc_kernel(tc, ff, attn_out, Wf, b_f, ln2_g, ln2_b
                     in_=x_grouped[m][:, j * width * PACK : (j + 1) * width * PACK],
                 )
 
-        def multiply(m, g):
+        def multiply(m, g, h):
             if g == 0:
-                acc[m] = [acc_pool.tile([P, BANK], F32, name="acc") for h in range(HALVES)]
+                acc[m, h] = acc_pool.tile([P, BANK], F32, name="acc")
             tokens = slice(g * P, (g + 1) * P)
-            for h in range(HALVES):
-                cols = slice(h * BANK, (h + 1) * BANK)
-                nc.tensor.matmul_mx(
-                    out=acc[m][h][:],
-                    lhsT=x_codes[m][:, tokens].bitcast(FP8X4),
-                    lhsT_scale=x_scales[m][:, tokens],
-                    rhs=w_codes[:, g, cols].bitcast(FP8X4),
-                    rhs_scale=w_scales[:, g, cols],
-                    start=(g == 0),
-                    stop=(g == PASSES - 1),
-                )
-
-        def add_residual_and_bias(m):
-            resid[m] = resid_pool.tile([P, N], F32, name="resid")
-            for h in range(HALVES):
-                cols = slice(h * BANK, (h + 1) * BANK)
-                bank = stage.tile([P, BANK], F32, name="bank")
-                nc.tensor.matmul(out=bank[:], lhsT=ident_bf16[:], rhs=attn_tile[m][:, cols], start=True, stop=False)
-                nc.tensor.matmul(out=bank[:], lhsT=pick[:, 0, :], rhs=vector_rows[:, cols], start=False, stop=True)
-                nc.scalar.copy(out=resid[m][:, cols], in_=bank[:])
-
-        def form_u(m):
-            u[m] = u_pool.tile([P, N], F32, name="u")
-            half_sums = stats.tile([P, HALVES], F32, name="half_sums")
-            for h in range(HALVES):
-                cols = slice(h * BANK, (h + 1) * BANK)
-                nc.vector.scalar_tensor_tensor(
-                    out=u[m][:, cols],
-                    in0=acc[m][h][:],
-                    scalar=1.0,
-                    in1=resid[m][:, cols],
-                    op0=ALU.mult,
-                    op1=ALU.add,
-                    accum_out=half_sums[:, h : h + 1],
-                )
-            neg_mean[m] = stats.tile([P, 1], F32, name="neg_mean")
-            nc.vector.tensor_scalar(
-                out=neg_mean[m][:],
-                in0=half_sums[:, 0:1],
-                scalar1=half_sums[:, 1:2],
-                scalar2=-1.0 / N,
-                op0=ALU.add,
-                op1=ALU.mult,
+            nc.tensor.matmul_mx(
+                out=acc[m, h][:],
+                lhsT=x_codes[m][:, tokens].bitcast(FP8X4),
+                lhsT_scale=x_scales[m][:, tokens],
+                rhs=w_codes[:, g, half(h)].bitcast(FP8X4),
+                rhs_scale=w_scales[:, g, half(h)],
+                start=(g == 0),
+                stop=(g == PASSES - 1),
             )
 
-        def deviation(m):
+        def add_residual_and_bias(m, h):
+            resid[m, h] = resid_pool.tile([P, BANK], F32, name="resid")
+            bank = stage.tile([P, BANK], F32, name="bank")
+            nc.tensor.matmul(out=bank[:], lhsT=ident_bf16[:], rhs=attn_tile[m][:, half(h)], start=True, stop=False)
+            nc.tensor.matmul(out=bank[:], lhsT=pick[:, 0, :], rhs=vector_rows[:, half(h)], start=False, stop=True)
+            nc.scalar.copy(out=resid[m, h][:], in_=bank[:])
+
+        def form_u(m, h):
+            if h == 0:
+                u[m] = u_pool.tile([P, N], F32, name="u")
+                half_sums[m] = stats.tile([P, HALVES], F32, name="half_sums")
+            nc.vector.scalar_tensor_tensor(
+                out=u[m][:, half(h)],
+                in0=acc[m, h][:],
+                scalar=1.0,
+                in1=resid[m, h][:],
+                op0=ALU.mult,
+                op1=ALU.add,
+                accum_out=half_sums[m][:, h : h + 1],
+            )
+
+        def statistics(m):
+            neg_mean[m] = stats.tile([P, 1], F32, name="neg_mean")
+            scaled = stats.tile([P, HALVES], F32, name="scaled")
+            nc.scalar.activation(
+                out=scaled[:], in_=half_sums[m][:], func=ACT.Identity, scale=-1.0 / N, accum_out=neg_mean[m][:]
+            )
             squares = scratch.tile([P, N], BF16, name="squares")
             sum_squares = stats.tile([P, 1], F32, name="sum_squares")
             nc.scalar.activation(
                 out=squares[:], in_=u[m][:], func=ACT.Square, bias=neg_mean[m][:], scale=1.0, accum_out=sum_squares[:]
             )
-            std[m] = stats.tile([P, 1], F32, name="std")
-            nc.scalar.activation(out=std[m][:], in_=sum_squares[:], func=ACT.Sqrt, bias=eps[:], scale=1.0 / N)
+            rstd[m] = stats.tile([P, 1], F32, name="rstd")
+            nc.scalar.activation(
+                out=rstd[m][:], in_=sum_squares[:], func=ACT.Abs_reciprocal_sqrt, bias=eps[:], scale=1.0 / N
+            )
 
         def centre_and_gain(m):
             y[m] = y_pool.tile([P, N], F32, name="y")
@@ -219,58 +219,139 @@ def tile_disentangledattention_pc_kernel(tc, ff, attn_out, Wf, b_f, ln2_g, ln2_b
             )
 
         def scale_shift_store(m):
-            rstd = stats.tile([P, 1], F32, name="rstd")
-            nc.vector.reciprocal(out=rstd[:], in_=std[m][:])
             nc.vector.scalar_tensor_tensor(
-                out=y[m][:], in0=y[m][:], scalar=rstd[:], in1=beta[:], op0=ALU.mult, op1=ALU.add
+                out=y[m][:], in0=y[m][:], scalar=rstd[m][:], in1=beta[:], op0=ALU.mult, op1=ALU.add
             )
             nc.sync.dma_start(out=out_rows[m * P : (m + 1) * P, :], in_=y[m][:])
 
-        for step in range(PASSES):
-            load_weights(step)
-            if step < EARLY_TILES:
-                load_tokens(step)
-            if step == 0:
-                spread_gain_and_shift()
-            regroup_weights(step)
-            if 1 <= step <= EARLY_TILES:
-                quantise_tokens(step - 1)
-            quantise_weights(step)
-            if step < EARLY_TILES:
-                for j in range(FILLS):
-                    transpose_tokens(step, j)
-            if step == PASSES - 1:
-                load_residual(0)
-                add_residual_and_bias(0)
-            for m in range(EARLY_TILES):
-                for g in range(PASSES):
-                    if max(m + 1, g) == step:
-                        multiply(m, g)
+        load_weights(0, 0)
+        load_tokens(0)
+        load_vectors()
+        load_weights(1, 0)
+        load_weights(2, 0)
+        load_tokens(1)
+        load_weights(3, 0)
+        load_weights(4, 0)
+        load_tokens(2)
+        later_loads = [
+            lambda: (load_weights(5, 0), load_residual(0)),
+            lambda: (load_weights(0, 1), load_residual(1)),
+            lambda: (load_weights(1, 1), load_residual(2)),
+            lambda: load_weights(2, 1),
+            lambda: load_weights(3, 1),
+            lambda: (load_tokens(3), load_weights(4, 1)),
+            lambda: (load_weights(5, 1), load_tokens(4)),
+        ]
 
-        for m in range(EARLY_TILES, TILES):
+        LAG = 0
+        NXT = 4
+        jobs = [("x", m, j) for m in range(EARLY_TILES) for j in range(FILLS)]
+        jobs += [("r", m, 0) for m in range(EARLY_TILES)]
+        jobs += [("r", m, 1) for m in range(EARLY_TILES)]
+        jobs += [("x", EARLY_TILES, j) for j in range(FILLS)]
+        if NXT == EARLY_TILES + 2:
+            jobs += [("x", EARLY_TILES + 1, j) for j in range(FILLS)]
+
+        STEPS = PASSES * HALVES
+        RATE = 6
+        JOB0 = 0
+        MXLAG = 1
+        ready_tiles = []
+        quantised = {}
+        formed = set()
+        todo = [(m, g, h) for h in range(HALVES) for m in range(EARLY_TILES) for g in range(PASSES)]
+        taken = 0
+        closed = {}
+        for step in range(STEPS + LAG):
+            h, g = divmod(step, PASSES)
+            if later_loads:
+                later_loads.pop(0)()
+            if step < STEPS:
+                regroup_weights(g, h)
+            if 1 <= step <= HALVES:
+                spread_gain_and_shift(step - 1)
+            if ready_tiles:
+                m = ready_tiles.pop(0)
+                quantise_tokens(m)
+                quantised[m] = step
+            else:
+                for m in range(EARLY_TILES):
+                    if m not in formed and closed.get((m, 0), STEPS) < step:
+                        form_u(m, 0)
+                        formed.add(m)
+                        break
+            if step >= LAG:
+                h, g = divmod(step - LAG, PASSES)
+                quantise_weights(g, h)
+            want = min(len(jobs) if step < STEPS - 1 else len(jobs), RATE * (step + 1) // 4 + JOB0) if step < STEPS - 1 + LAG else len(jobs)
+            while taken < want:
+                kind, m, j = jobs[taken]
+                taken += 1
+                if kind == "x":
+                    transpose_tokens(m, j)
+                    if j == FILLS - 1:
+                        ready_tiles.append(m)
+                else:
+                    add_residual_and_bias(m, j)
+            for item in list(todo):
+                m, gg, hh = item
+                if hh * PASSES + gg < step - LAG + 1 - MXLAG and quantised.get(m, STEPS + 2) < step + 1 - MXLAG and (hh == 0 or m in formed):
+                    multiply(m, gg, hh)
+                    todo.remove(item)
+                    if gg == PASSES - 1:
+                        closed[m, hh] = step
+
+        load_residual(EARLY_TILES)
+        for m in range(EARLY_TILES + 2, TILES):
             load_tokens(m)
-            load_residual(m - EARLY_TILES + 1)
-        for m in range(TILES - EARLY_TILES + 1, TILES):
-            load_residual(m)
-        for j in range(FILLS):
-            transpose_tokens(EARLY_TILES, j)
+            load_residual(m - 1)
+        load_residual(TILES - 1)
 
-        for s in range(TILES):
-            multiplied = s + EARLY_TILES
-            transposed = multiplied + 1
-            if s + 1 < TILES:
-                add_residual_and_bias(s + 1)
-            form_u(s)
-            deviation(s)
-            if s >= 1:
-                scale_shift_store(s - 1)
-            centre_and_gain(s)
-            if multiplied < TILES:
-                quantise_tokens(multiplied)
-            if transposed < TILES:
-                for j in range(FILLS):
-                    transpose_tokens(transposed, j)
-            if multiplied < TILES:
+        for m in range(EARLY_TILES):
+            if m not in formed:
+                form_u(m, 0)
+        for m, gg, hh in todo:
+            multiply(m, gg, hh)
+
+        units = [(m, h) for m in range(EARLY_TILES, TILES) for h in range(HALVES)]
+        state = {"free": ACC_BANKS - EARLY_TILES}
+        done_x = [m for m in quantised]
+
+        def multiply_units():
+            while units and state["free"] > 0 and units[0][0] in done_x:
+                m, h = units.pop(0)
                 for g in range(PASSES):
-                    multiply(multiplied, g)
-        scale_shift_store(TILES - 1)
+                    multiply(m, g, h)
+                state["free"] -= 1
+
+        for m in ready_tiles:
+            quantise_tokens(m)
+            done_x.append(m)
+        ready_tiles.clear()
+        nxt = NXT
+        multiply_units()
+        for t in range(TILES + 2):
+            pending = list(ready_tiles)
+            ready_tiles.clear()
+            if t < TILES:
+                for h in range(HALVES):
+                    if h == 1 or t >= EARLY_TILES:
+                        form_u(t, h)
+                        state["free"] += 1
+                statistics(t)
+            if nxt < TILES:
+                for j in range(FILLS):
+                    transpose_tokens(nxt, j)
+                ready_tiles.append(nxt)
+                nxt += 1
+            if EARLY_TILES <= t + 2 < TILES:
+                for h in range(HALVES):
+                    add_residual_and_bias(t + 2, h)
+            if t >= 2:
+                scale_shift_store(t - 2)
+            if 1 <= t <= TILES:
+                centre_and_gain(t - 1)
+            for m in pending:
+                quantise_tokens(m)
+                done_x.append(m)
+            multiply_units()

@@ -28,7 +28,7 @@ PASSES_PER_FILL = PASSES // FILLS
 EARLY_TILES = 3
 ACC_BANKS = 4
 STAGE_BANKS = 8 - ACC_BANKS
-W_VECTOR_COLS = 352
+W_VECTOR_COLS = 320
 
 FLOPS = 2 * TOKENS * K * N
 
@@ -54,7 +54,7 @@ def tile_disentangledattention_pc_kernel(tc, ff, attn_out, Wf, b_f, ln2_g, ln2_b
         stats = ctx.enter_context(tc.tile_pool(name="stats", bufs=TILES))
         acc_pool = ctx.enter_context(tc.psum_pool(name="acc", bufs=ACC_BANKS))
         stage = ctx.enter_context(tc.psum_pool(name="stage", bufs=STAGE_BANKS))
-        ctx.enter_context(tc.manual_schedule())
+        ctx.enter_context(tc.manual_schedule(engines={mybir.EngineType.DVE, mybir.EngineType.SP}))
 
         ident_words = const.tile([P, P], F32)
         make_identity(nc, ident_words[:])
@@ -97,9 +97,11 @@ def tile_disentangledattention_pc_kernel(tc, ff, attn_out, Wf, b_f, ln2_g, ln2_b
         def half(h):
             return slice(h * BANK, (h + 1) * BANK)
 
-        def load_tokens(m):
-            ff_tile[m] = ff_pool.tile([P, K], BF16, name="ff_tile")
-            nc.sync.dma_start(out=ff_tile[m][:], in_=ff_rows[m * P : (m + 1) * P, :])
+        def load_tokens(m, pieces=(slice(0, K),)):
+            if m not in ff_tile:
+                ff_tile[m] = ff_pool.tile([P, K], BF16, name="ff_tile")
+            for cols in pieces:
+                nc.sync.dma_start(out=ff_tile[m][:, cols], in_=ff_rows[m * P : (m + 1) * P, cols])
 
         def load_residual(m):
             attn_tile[m] = attn_pool.tile([P, N], BF16, name="attn_tile")
@@ -218,14 +220,22 @@ def tile_disentangledattention_pc_kernel(tc, ff, attn_out, Wf, b_f, ln2_g, ln2_b
                 out=y[m][:], in0=u[m][:], scalar=neg_mean[m][:], in1=gamma[:], op0=ALU.add, op1=ALU.mult
             )
 
-        def scale_shift_store(m):
-            nc.vector.scalar_tensor_tensor(
-                out=y[m][:], in0=y[m][:], scalar=rstd[m][:], in1=beta[:], op0=ALU.mult, op1=ALU.add
-            )
-            nc.sync.dma_start(out=out_rows[m * P : (m + 1) * P, :], in_=y[m][:])
+        def scale_shift_store(m, pieces=(slice(0, N),)):
+            for cols in pieces:
+                nc.vector.scalar_tensor_tensor(
+                    out=y[m][:, cols],
+                    in0=y[m][:, cols],
+                    scalar=rstd[m][:],
+                    in1=beta[:, cols],
+                    op0=ALU.mult,
+                    op1=ALU.add,
+                )
+                nc.sync.dma_start(out=out_rows[m * P : (m + 1) * P, cols], in_=y[m][:, cols])
 
+        fills = [slice(j * K // FILLS, (j + 1) * K // FILLS) for j in range(FILLS)]
+        load_tokens(0, fills[:1])
         load_weights(0, 0)
-        load_tokens(0)
+        load_tokens(0, fills[1:])
         load_vectors()
         load_weights(1, 0)
         load_weights(2, 0)
@@ -333,9 +343,17 @@ def tile_disentangledattention_pc_kernel(tc, ff, attn_out, Wf, b_f, ln2_g, ln2_b
         for t in range(TILES + 2):
             pending = list(ready_tiles)
             ready_tiles.clear()
+            if 2 <= t < TILES:
+                scale_shift_store(t - 2)
+            if t == TILES + 1:
+                scale_shift_store(TILES - 1, [slice(h * BANK, (h + 1) * BANK) for h in range(HALVES)])
+            if 1 <= t <= TILES:
+                centre_and_gain(t - 1)
             if t < TILES:
                 for h in range(HALVES):
                     if h == 1 or t >= EARLY_TILES:
+                        if t == TILES - 1 and h == 1:
+                            scale_shift_store(TILES - 2)
                         form_u(t, h)
                         state["free"] += 1
                 statistics(t)
@@ -347,10 +365,6 @@ def tile_disentangledattention_pc_kernel(tc, ff, attn_out, Wf, b_f, ln2_g, ln2_b
             if EARLY_TILES <= t + 2 < TILES:
                 for h in range(HALVES):
                     add_residual_and_bias(t + 2, h)
-            if t >= 2:
-                scale_shift_store(t - 2)
-            if 1 <= t <= TILES:
-                centre_and_gain(t - 1)
             for m in pending:
                 quantise_tokens(m)
                 done_x.append(m)

@@ -54,7 +54,7 @@ def tile_disentangledattention_pc_kernel(tc, ff, attn_out, Wf, b_f, ln2_g, ln2_b
         stats = ctx.enter_context(tc.tile_pool(name="stats", bufs=TILES))
         acc_pool = ctx.enter_context(tc.psum_pool(name="acc", bufs=ACC_BANKS))
         stage = ctx.enter_context(tc.psum_pool(name="stage", bufs=STAGE_BANKS))
-        ctx.enter_context(tc.manual_schedule(engines={mybir.EngineType.DVE, mybir.EngineType.SP}))
+        ctx.enter_context(tc.manual_schedule())
 
         ident_words = const.tile([P, P], F32)
         make_identity(nc, ident_words[:])

@@ -45,6 +45,7 @@ def tile_disentangledattention_pc_kernel(tc, ff, attn_out, Wf, b_f, ln2_g, ln2_b
         attn_pool = ctx.enter_context(tc.tile_pool(name="attn", bufs=TILES))
         w_raw_pool = ctx.enter_context(tc.tile_pool(name="w_raw", bufs=6))
         w_grouped_pool = ctx.enter_context(tc.tile_pool(name="w_grouped", bufs=3))
+        arranged_pool = ctx.enter_context(tc.tile_pool(name="arranged", bufs=1))
         x_grouped_pool = ctx.enter_context(tc.tile_pool(name="x_grouped", bufs=2))
         x_pool = ctx.enter_context(tc.tile_pool(name="x", bufs=EARLY_TILES + 3))
         resid_pool = ctx.enter_context(tc.tile_pool(name="resid", bufs=6))
@@ -91,7 +92,7 @@ def tile_disentangledattention_pc_kernel(tc, ff, attn_out, Wf, b_f, ln2_g, ln2_b
         w_scales = const.tile([P, PASSES, N], U8, align_bytes=64)
 
         ff_tile, attn_tile, w_raw, w_grouped = {}, {}, {}, {}
-        x_grouped, x_codes, x_scales = {}, {}, {}
+        arranged, x_grouped, x_codes, x_scales = {}, {}, {}, {}
         acc, resid, u, y, half_sums, neg_mean, rstd = {}, {}, {}, {}, {}, {}, {}
 
         def half(h):
@@ -134,17 +135,26 @@ def tile_disentangledattention_pc_kernel(tc, ff, attn_out, Wf, b_f, ln2_g, ln2_b
                 in_=w_grouped[g, h][:].rearrange("p c t -> p (c t)"),
             )
 
+        def arrange_tokens(m):
+            arranged[m] = arranged_pool.tile([P, K // 2], F32, name="arranged")
+            nc.scalar.copy(
+                out=arranged[m][:].rearrange("p (g u w) -> p g u w", u=2, w=P),
+                in_=ff_tile[m][:].bitcast(F32).rearrange("p (g w u) -> p g u w", u=2, w=P),
+            )
+
         def transpose_tokens(m, j):
             if j == 0:
                 x_grouped[m] = x_grouped_pool.tile([P, PASSES * P * PACK], BF16, name="x_grouped", align_bytes=64)
-            words = ff_tile[m][:].bitcast(F32)
+            words = arranged[m][:] if m in arranged else ff_tile[m][:].bitcast(F32)
             bank = stage.tile([P, BANK], F32, name="bank")
             for q in range(BANK // P):
                 g, u_slot = divmod(q, 2)
                 first = j * BANK + g * 2 * P
-                nc.tensor.transpose(
-                    bank[:, q * P : (q + 1) * P], words[:, first + u_slot : first + 2 * P : 2], ident_words[:]
-                )
+                if m in arranged:
+                    taken_words = words[:, first + u_slot * P : first + (u_slot + 1) * P]
+                else:
+                    taken_words = words[:, first + u_slot : first + 2 * P : 2]
+                nc.tensor.transpose(bank[:, q * P : (q + 1) * P], taken_words, ident_words[:])
             nc.scalar.copy(
                 out=x_grouped[m][:].bitcast(F32)[:, j * BANK : (j + 1) * BANK].rearrange(
                     "p (g r u) -> p g r u", g=PASSES_PER_FILL, u=2
@@ -204,6 +214,8 @@ def tile_disentangledattention_pc_kernel(tc, ff, attn_out, Wf, b_f, ln2_g, ln2_b
             nc.scalar.activation(
                 out=scaled[:], in_=half_sums[m][:], func=ACT.Identity, scale=-1.0 / N, accum_out=neg_mean[m][:]
             )
+
+        def square(m):
             squares = scratch.tile([P, N], BF16, name="squares")
             sum_squares = stats.tile([P, 1], F32, name="sum_squares")
             nc.scalar.activation(
@@ -232,53 +244,50 @@ def tile_disentangledattention_pc_kernel(tc, ff, attn_out, Wf, b_f, ln2_g, ln2_b
                 )
                 nc.sync.dma_start(out=out_rows[m * P : (m + 1) * P, cols], in_=y[m][:, cols])
 
-        fills = [slice(j * K // FILLS, (j + 1) * K // FILLS) for j in range(FILLS)]
-        load_tokens(0, fills[:1])
-        load_weights(0, 0)
-        load_tokens(0, fills[1:])
-        load_vectors()
-        load_weights(1, 0)
-        load_weights(2, 0)
-        load_tokens(1)
-        load_weights(3, 0)
-        load_weights(4, 0)
-        load_tokens(2)
-        later_loads = [
-            lambda: (load_weights(5, 0), load_residual(0)),
-            lambda: (load_weights(0, 1), load_residual(1)),
-            lambda: (load_weights(1, 1), load_residual(2)),
-            lambda: load_weights(2, 1),
-            lambda: load_weights(3, 1),
-            lambda: (load_tokens(3), load_weights(4, 1)),
-            lambda: (load_weights(5, 1), load_tokens(4)),
-        ]
-
         LAG = 0
         NXT = 4
-        jobs = [("x", m, j) for m in range(EARLY_TILES) for j in range(FILLS)]
-        jobs += [("r", m, 0) for m in range(EARLY_TILES)]
-        jobs += [("r", m, 1) for m in range(EARLY_TILES)]
-        jobs += [("x", EARLY_TILES, j) for j in range(FILLS)]
-        if NXT == EARLY_TILES + 2:
-            jobs += [("x", EARLY_TILES + 1, j) for j in range(FILLS)]
+        fills = [slice(j * K // FILLS, (j + 1) * K // FILLS) for j in range(FILLS)]
+        order = "f00 w0 f012 v w1 w2 x1 w3 w4 x2 w5 a0 w6 a1 w7 a2 w8 w9 x3 w10 w11 x4 a3 x5 a4 x6 a5 x7 a6 a7".split()
+
+        def load_until(w_last):
+            while order:
+                kind, n = order[0][0], order[0][1:]
+                if kind == "w" and int(n) > w_last:
+                    return
+                order.pop(0)
+                if kind == "w":
+                    load_weights(int(n) % PASSES, int(n) // PASSES)
+                elif kind == "x":
+                    load_tokens(int(n))
+                elif kind == "f":
+                    load_tokens(int(n[0]), [fills[int(c)] for c in n[1:]])
+                elif kind == "a":
+                    load_residual(int(n))
+                else:
+                    load_vectors()
+
+        load_until(4)
+        jobs = []
+        for item in "x0 x1 x2 r00 r10 r20 r01 r11 r21 x3".split():
+            kind, m = item[0], int(item[1])
+            if kind == "x":
+                jobs += [("x", m, j) for j in range(FILLS)]
+            else:
+                jobs.append(("r", m, int(item[2])))
+        counts = [3,0,0,3,0,3,1,1,1,3,0,3]
 
         STEPS = PASSES * HALVES
-        RATE = 6
-        JOB0 = 0
-        MXLAG = 1
         ready_tiles = []
         quantised = {}
         formed = set()
         todo = [(m, g, h) for h in range(HALVES) for m in range(EARLY_TILES) for g in range(PASSES)]
         taken = 0
         closed = {}
-        for step in range(STEPS + LAG):
+        for step in range(STEPS):
             h, g = divmod(step, PASSES)
-            if later_loads:
-                later_loads.pop(0)()
-            if step < STEPS:
-                regroup_weights(g, h)
-            if 1 <= step <= HALVES:
+            load_until(step + 5)
+            regroup_weights(g, h)
+            if 1 <= step < 1 + HALVES:
                 spread_gain_and_shift(step - 1)
             if ready_tiles:
                 m = ready_tiles.pop(0)
@@ -290,10 +299,8 @@ def tile_disentangledattention_pc_kernel(tc, ff, attn_out, Wf, b_f, ln2_g, ln2_b
                         form_u(m, 0)
                         formed.add(m)
                         break
-            if step >= LAG:
-                h, g = divmod(step - LAG, PASSES)
-                quantise_weights(g, h)
-            want = min(len(jobs) if step < STEPS - 1 else len(jobs), RATE * (step + 1) // 4 + JOB0) if step < STEPS - 1 + LAG else len(jobs)
+            quantise_weights(g, h)
+            want = min(len(jobs), taken + counts[step])
             while taken < want:
                 kind, m, j = jobs[taken]
                 taken += 1
@@ -305,17 +312,12 @@ def tile_disentangledattention_pc_kernel(tc, ff, attn_out, Wf, b_f, ln2_g, ln2_b
                     add_residual_and_bias(m, j)
             for item in list(todo):
                 m, gg, hh = item
-                if hh * PASSES + gg < step - LAG + 1 - MXLAG and quantised.get(m, STEPS + 2) < step + 1 - MXLAG and (hh == 0 or m in formed):
+                if hh * PASSES + gg < step + 0 and quantised.get(m, STEPS) < step + 0 and (hh == 0 or m in formed):
                     multiply(m, gg, hh)
                     todo.remove(item)
                     if gg == PASSES - 1:
                         closed[m, hh] = step
-
-        load_residual(EARLY_TILES)
-        for m in range(EARLY_TILES + 2, TILES):
-            load_tokens(m)
-            load_residual(m - 1)
-        load_residual(TILES - 1)
+        load_until(99)
 
         for m in range(EARLY_TILES):
             if m not in formed:
@@ -323,6 +325,8 @@ def tile_disentangledattention_pc_kernel(tc, ff, attn_out, Wf, b_f, ln2_g, ln2_b
         for m, gg, hh in todo:
             multiply(m, gg, hh)
 
+        TSLOT = {0: (4,), 1: (5,), 2: (6,), 4: (7,)}
+        PSLOT = {3: (7,)}
         units = [(m, h) for m in range(EARLY_TILES, TILES) for h in range(HALVES)]
         state = {"free": ACC_BANKS - EARLY_TILES}
         done_x = [m for m in quantised]
@@ -357,14 +361,19 @@ def tile_disentangledattention_pc_kernel(tc, ff, attn_out, Wf, b_f, ln2_g, ln2_b
                         form_u(t, h)
                         state["free"] += 1
                 statistics(t)
-            if nxt < TILES:
+                if not False:
+                    square(t)
+            for m in TSLOT.get(t, ()):
                 for j in range(FILLS):
-                    transpose_tokens(nxt, j)
-                ready_tiles.append(nxt)
-                nxt += 1
+                    transpose_tokens(m, j)
+                ready_tiles.append(m)
             if EARLY_TILES <= t + 2 < TILES:
                 for h in range(HALVES):
                     add_residual_and_bias(t + 2, h)
+            if False and t < TILES:
+                square(t)
+            for m in PSLOT.get(t, ()):
+                arrange_tokens(m)
             for m in pending:
                 quantise_tokens(m)
                 done_x.append(m)

@@ -28,7 +28,7 @@ PASSES_PER_FILL = PASSES // FILLS
 EARLY_TILES = 3
 ACC_BANKS = 4
 STAGE_BANKS = 8 - ACC_BANKS
-W_VECTOR_COLS = 320
+W_VECTOR_COLS = 304
 
 FLOPS = 2 * TOKENS * K * N
 
@@ -356,13 +356,12 @@ def tile_disentangledattention_pc_kernel(tc, ff, attn_out, Wf, b_f, ln2_g, ln2_b
             if t < TILES:
                 for h in range(HALVES):
                     if h == 1 or t >= EARLY_TILES:
-                        if t == TILES - 1 and h == 1:
-                            scale_shift_store(TILES - 2)
                         form_u(t, h)
                         state["free"] += 1
                 statistics(t)
-                if not False:
-                    square(t)
+                square(t)
+                if t == TILES - 1:
+                    scale_shift_store(TILES - 2)
             for m in TSLOT.get(t, ()):
                 for j in range(FILLS):
                     transpose_tokens(m, j)

@@ -22,13 +22,18 @@ PASSES = K // K_PASS
 TILES = TOKENS // P
 BANK = 512
 HALVES = N // BANK
+STEPS = PASSES * HALVES
 FILLS = K // 2 // BANK
 PASSES_PER_FILL = PASSES // FILLS
 
 EARLY_TILES = 3
-ACC_BANKS = 4
+ACC_BANKS = EARLY_TILES + 1
 STAGE_BANKS = 8 - ACC_BANKS
 W_VECTOR_COLS = 304
+TOKENS_BEHIND = (-1, 2, 4, STEPS - 2)
+TRANSPOSE_STEP = tuple(step + 1 for step in TOKENS_BEHIND)
+RESIDUAL_STEP = PASSES
+LAST = TILES - 1
 
 FLOPS = 2 * TOKENS * K * N
 
@@ -43,12 +48,12 @@ def tile_disentangledattention_pc_kernel(tc, ff, attn_out, Wf, b_f, ln2_g, ln2_b
         const = ctx.enter_context(tc.tile_pool(name="const", bufs=1))
         ff_pool = ctx.enter_context(tc.tile_pool(name="ff", bufs=TILES))
         attn_pool = ctx.enter_context(tc.tile_pool(name="attn", bufs=TILES))
-        w_raw_pool = ctx.enter_context(tc.tile_pool(name="w_raw", bufs=6))
+        w_raw_pool = ctx.enter_context(tc.tile_pool(name="w_raw", bufs=PASSES))
         w_grouped_pool = ctx.enter_context(tc.tile_pool(name="w_grouped", bufs=3))
         arranged_pool = ctx.enter_context(tc.tile_pool(name="arranged", bufs=1))
         x_grouped_pool = ctx.enter_context(tc.tile_pool(name="x_grouped", bufs=2))
         x_pool = ctx.enter_context(tc.tile_pool(name="x", bufs=EARLY_TILES + 3))
-        resid_pool = ctx.enter_context(tc.tile_pool(name="resid", bufs=6))
+        resid_pool = ctx.enter_context(tc.tile_pool(name="resid", bufs=EARLY_TILES * HALVES))
         u_pool = ctx.enter_context(tc.tile_pool(name="u", bufs=EARLY_TILES + 2))
         y_pool = ctx.enter_context(tc.tile_pool(name="y", bufs=3))
         scratch = ctx.enter_context(tc.tile_pool(name="scratch", bufs=2))
@@ -56,6 +61,9 @@ def tile_disentangledattention_pc_kernel(tc, ff, attn_out, Wf, b_f, ln2_g, ln2_b
         acc_pool = ctx.enter_context(tc.psum_pool(name="acc", bufs=ACC_BANKS))
         stage = ctx.enter_context(tc.psum_pool(name="stage", bufs=STAGE_BANKS))
         ctx.enter_context(tc.manual_schedule())
+
+        def half(h):
+            return slice(h * BANK, (h + 1) * BANK)
 
         ident_words = const.tile([P, P], F32)
         make_identity(nc, ident_words[:])
@@ -71,22 +79,8 @@ def tile_disentangledattention_pc_kernel(tc, ff, attn_out, Wf, b_f, ln2_g, ln2_b
             nc.vector.memset(pick[32 * j : 32 * j + 1, j, :], 1.0)
         gamma = const.tile([P, N], F32)
         beta = const.tile([P, N], F32)
-
         warm = const.tile([P, 1], F32)
         nc.scalar.activation(out=warm[:], in_=eps[:], func=ACT.Abs_reciprocal_sqrt)
-
-        def load_vectors():
-            for j, vec in enumerate((b_f, ln2_g, ln2_b)):
-                nc.sync.dma_start(out=vector_rows[32 * j : 32 * j + 1, :], in_=vec.rearrange("(o n) -> o n", o=1))
-
-        def spread_gain_and_shift(h):
-            cols = slice(h * BANK, (h + 1) * BANK)
-            gamma_bank = stage.tile([P, BANK], F32, name="bank")
-            nc.tensor.matmul(out=gamma_bank[:], lhsT=pick[:, 1, :], rhs=vector_rows[:, cols], start=True, stop=True)
-            nc.vector.tensor_copy(out=gamma[:, cols], in_=gamma_bank[:])
-            beta_bank = stage.tile([P, BANK], F32, name="bank")
-            nc.tensor.matmul(out=beta_bank[:], lhsT=pick[:, 2, :], rhs=vector_rows[:, cols], start=True, stop=True)
-            nc.scalar.copy(out=beta[:, cols], in_=beta_bank[:])
 
         w_codes = const.tile([P, PASSES, N], U32, align_bytes=64)
         w_scales = const.tile([P, PASSES, N], U8, align_bytes=64)
@@ -94,9 +88,6 @@ def tile_disentangledattention_pc_kernel(tc, ff, attn_out, Wf, b_f, ln2_g, ln2_b
         ff_tile, attn_tile, w_raw, w_grouped = {}, {}, {}, {}
         arranged, x_grouped, x_codes, x_scales = {}, {}, {}, {}
         acc, resid, u, y, half_sums, neg_mean, rstd = {}, {}, {}, {}, {}, {}, {}
-
-        def half(h):
-            return slice(h * BANK, (h + 1) * BANK)
 
         def load_tokens(m, pieces=(slice(0, K),)):
             if m not in ff_tile:
@@ -114,6 +105,18 @@ def tile_disentangledattention_pc_kernel(tc, ff, attn_out, Wf, b_f, ln2_g, ln2_b
                 out=w_raw[g, h][:],
                 in_=Wf[g * K_PASS : (g + 1) * K_PASS, half(h)].rearrange("(p t) c -> p t c", t=PACK),
             )
+
+        def load_vectors():
+            for j, vec in enumerate((b_f, ln2_g, ln2_b)):
+                nc.sync.dma_start(out=vector_rows[32 * j : 32 * j + 1, :], in_=vec.rearrange("(o n) -> o n", o=1))
+
+        def spread_gain_and_shift(h):
+            gamma_bank = stage.tile([P, BANK], F32, name="bank")
+            nc.tensor.matmul(out=gamma_bank[:], lhsT=pick[:, 1, :], rhs=vector_rows[:, half(h)], start=True, stop=True)
+            nc.vector.tensor_copy(out=gamma[:, half(h)], in_=gamma_bank[:])
+            beta_bank = stage.tile([P, BANK], F32, name="bank")
+            nc.tensor.matmul(out=beta_bank[:], lhsT=pick[:, 2, :], rhs=vector_rows[:, half(h)], start=True, stop=True)
+            nc.scalar.copy(out=beta[:, half(h)], in_=beta_bank[:])
 
         def regroup_weights(g, h):
             w_grouped[g, h] = w_grouped_pool.tile([P, BANK, PACK], BF16, name="w_grouped", align_bytes=64)
@@ -142,25 +145,27 @@ def tile_disentangledattention_pc_kernel(tc, ff, attn_out, Wf, b_f, ln2_g, ln2_b
                 in_=ff_tile[m][:].bitcast(F32).rearrange("p (g w u) -> p g u w", u=2, w=P),
             )
 
-        def transpose_tokens(m, j):
-            if j == 0:
-                x_grouped[m] = x_grouped_pool.tile([P, PASSES * P * PACK], BF16, name="x_grouped", align_bytes=64)
-            words = arranged[m][:] if m in arranged else ff_tile[m][:].bitcast(F32)
-            bank = stage.tile([P, BANK], F32, name="bank")
-            for q in range(BANK // P):
-                g, u_slot = divmod(q, 2)
-                first = j * BANK + g * 2 * P
-                if m in arranged:
-                    taken_words = words[:, first + u_slot * P : first + (u_slot + 1) * P]
-                else:
-                    taken_words = words[:, first + u_slot : first + 2 * P : 2]
-                nc.tensor.transpose(bank[:, q * P : (q + 1) * P], taken_words, ident_words[:])
-            nc.scalar.copy(
-                out=x_grouped[m][:].bitcast(F32)[:, j * BANK : (j + 1) * BANK].rearrange(
-                    "p (g r u) -> p g r u", g=PASSES_PER_FILL, u=2
-                ),
-                in_=bank[:].rearrange("p (g u r) -> p g r u", g=PASSES_PER_FILL, u=2),
-            )
+        def words_of(m, g, slot):
+            if m in arranged:
+                first = (2 * g + slot) * P
+                return arranged[m][:, first : first + P]
+            first = 2 * g * P + slot
+            return ff_tile[m][:].bitcast(F32)[:, first : 2 * (g + 1) * P : 2]
+
+        def transpose_tokens(m):
+            x_grouped[m] = x_grouped_pool.tile([P, PASSES * P * PACK], BF16, name="x_grouped", align_bytes=64)
+            for j in range(FILLS):
+                bank = stage.tile([P, BANK], F32, name="bank")
+                for q in range(BANK // P):
+                    i, slot = divmod(q, 2)
+                    words = words_of(m, j * PASSES_PER_FILL + i, slot)
+                    nc.tensor.transpose(bank[:, q * P : (q + 1) * P], words, ident_words[:])
+                nc.scalar.copy(
+                    out=x_grouped[m][:].bitcast(F32)[:, j * BANK : (j + 1) * BANK].rearrange(
+                        "p (g r u) -> p g r u", g=PASSES_PER_FILL, u=2
+                    ),
+                    in_=bank[:].rearrange("p (g u r) -> p g r u", g=PASSES_PER_FILL, u=2),
+                )
 
         def quantise_tokens(m):
             x_codes[m] = x_pool.tile([P, PASSES * P], U32, name="x_codes", align_bytes=64)
@@ -214,8 +219,6 @@ def tile_disentangledattention_pc_kernel(tc, ff, attn_out, Wf, b_f, ln2_g, ln2_b
             nc.scalar.activation(
                 out=scaled[:], in_=half_sums[m][:], func=ACT.Identity, scale=-1.0 / N, accum_out=neg_mean[m][:]
             )
-
-        def square(m):
             squares = scratch.tile([P, N], BF16, name="squares")
             sum_squares = stats.tile([P, 1], F32, name="sum_squares")
             nc.scalar.activation(
@@ -244,136 +247,90 @@ def tile_disentangledattention_pc_kernel(tc, ff, attn_out, Wf, b_f, ln2_g, ln2_b
                 )
                 nc.sync.dma_start(out=out_rows[m * P : (m + 1) * P, cols], in_=y[m][:, cols])
 
-        LAG = 0
-        NXT = 4
         fills = [slice(j * K // FILLS, (j + 1) * K // FILLS) for j in range(FILLS)]
-        order = "f00 w0 f012 v w1 w2 x1 w3 w4 x2 w5 a0 w6 a1 w7 a2 w8 w9 x3 w10 w11 x4 a3 x5 a4 x6 a5 x7 a6 a7".split()
+        load_tokens(0, fills[:1])
+        load_weights(0, 0)
+        load_tokens(0, fills[1:])
+        load_vectors()
+        for g in range(1, PASSES):
+            load_weights(g, 0)
+            if g in TOKENS_BEHIND:
+                load_tokens(TOKENS_BEHIND.index(g))
+        load_residual(0)
 
-        def load_until(w_last):
-            while order:
-                kind, n = order[0][0], order[0][1:]
-                if kind == "w" and int(n) > w_last:
-                    return
-                order.pop(0)
-                if kind == "w":
-                    load_weights(int(n) % PASSES, int(n) // PASSES)
-                elif kind == "x":
-                    load_tokens(int(n))
-                elif kind == "f":
-                    load_tokens(int(n[0]), [fills[int(c)] for c in n[1:]])
-                elif kind == "a":
-                    load_residual(int(n))
-                else:
-                    load_vectors()
+        def step_of_product(m, g, h):
+            ready = max(PASSES * h + g, TRANSPOSE_STEP[m] + 1) + 1
+            return max(ready, RESIDUAL_STEP + m + 1) if h else ready
 
-        load_until(4)
-        jobs = []
-        for item in "x0 x1 x2 r00 r10 r20 r01 r11 r21 x3".split():
-            kind, m = item[0], int(item[1])
-            if kind == "x":
-                jobs += [("x", m, j) for j in range(FILLS)]
-            else:
-                jobs.append(("r", m, int(item[2])))
-        counts = [3,0,0,3,0,3,1,1,1,3,0,3]
-
-        STEPS = PASSES * HALVES
-        ready_tiles = []
-        quantised = {}
-        formed = set()
-        todo = [(m, g, h) for h in range(HALVES) for m in range(EARLY_TILES) for g in range(PASSES)]
-        taken = 0
-        closed = {}
-        for step in range(STEPS):
+        early_products = [(m, g, h) for h in range(HALVES) for m in range(EARLY_TILES) for g in range(PASSES)]
+        for step in range(STEPS + 1):
             h, g = divmod(step, PASSES)
-            load_until(step + 5)
-            regroup_weights(g, h)
-            if 1 <= step < 1 + HALVES:
+            if 1 <= step <= PASSES:
+                load_weights(step - 1, 1)
+                if step < EARLY_TILES:
+                    load_residual(step)
+                if step - 1 + PASSES in TOKENS_BEHIND:
+                    load_tokens(TOKENS_BEHIND.index(step - 1 + PASSES))
+            if step == PASSES:
+                for m in range(EARLY_TILES + 1, TILES):
+                    load_tokens(m)
+                    load_residual(m - 1)
+                load_residual(LAST)
+            if step < STEPS:
+                regroup_weights(g, h)
+            if 1 <= step <= HALVES:
                 spread_gain_and_shift(step - 1)
-            if ready_tiles:
-                m = ready_tiles.pop(0)
-                quantise_tokens(m)
-                quantised[m] = step
-            else:
+            if step - 1 in TRANSPOSE_STEP:
+                quantise_tokens(TRANSPOSE_STEP.index(step - 1))
+            if 0 <= step - 1 - RESIDUAL_STEP < EARLY_TILES:
+                form_u(step - 1 - RESIDUAL_STEP, 0)
+            if step < STEPS:
+                quantise_weights(g, h)
+            if step in TRANSPOSE_STEP:
+                transpose_tokens(TRANSPOSE_STEP.index(step))
+            if 0 <= step - RESIDUAL_STEP < EARLY_TILES:
+                add_residual_and_bias(step - RESIDUAL_STEP, 0)
+            if step == RESIDUAL_STEP + EARLY_TILES:
                 for m in range(EARLY_TILES):
-                    if m not in formed and closed.get((m, 0), STEPS) < step:
-                        form_u(m, 0)
-                        formed.add(m)
-                        break
-            quantise_weights(g, h)
-            want = min(len(jobs), taken + counts[step])
-            while taken < want:
-                kind, m, j = jobs[taken]
-                taken += 1
-                if kind == "x":
-                    transpose_tokens(m, j)
-                    if j == FILLS - 1:
-                        ready_tiles.append(m)
-                else:
-                    add_residual_and_bias(m, j)
-            for item in list(todo):
-                m, gg, hh = item
-                if hh * PASSES + gg < step + 0 and quantised.get(m, STEPS) < step + 0 and (hh == 0 or m in formed):
+                    add_residual_and_bias(m, 1)
+            for m, gg, hh in early_products:
+                if step_of_product(m, gg, hh) == step:
                     multiply(m, gg, hh)
-                    todo.remove(item)
-                    if gg == PASSES - 1:
-                        closed[m, hh] = step
-        load_until(99)
 
-        for m in range(EARLY_TILES):
-            if m not in formed:
-                form_u(m, 0)
-        for m, gg, hh in todo:
-            multiply(m, gg, hh)
+        later_products = [(m, h) for m in range(EARLY_TILES, TILES) for h in range(HALVES)]
 
-        TSLOT = {0: (4,), 1: (5,), 2: (6,), 4: (7,)}
-        PSLOT = {3: (7,)}
-        units = [(m, h) for m in range(EARLY_TILES, TILES) for h in range(HALVES)]
-        state = {"free": ACC_BANKS - EARLY_TILES}
-        done_x = [m for m in quantised]
-
-        def multiply_units():
-            while units and state["free"] > 0 and units[0][0] in done_x:
-                m, h = units.pop(0)
+        def multiply_next():
+            if later_products:
+                m, h = later_products.pop(0)
                 for g in range(PASSES):
                     multiply(m, g, h)
-                state["free"] -= 1
 
-        for m in ready_tiles:
-            quantise_tokens(m)
-            done_x.append(m)
-        ready_tiles.clear()
-        nxt = NXT
-        multiply_units()
-        for t in range(TILES + 2):
-            pending = list(ready_tiles)
-            ready_tiles.clear()
-            if 2 <= t < TILES:
+        multiply_next()
+        for t in range(TILES):
+            if t >= 2:
                 scale_shift_store(t - 2)
-            if t == TILES + 1:
-                scale_shift_store(TILES - 1, [slice(h * BANK, (h + 1) * BANK) for h in range(HALVES)])
-            if 1 <= t <= TILES:
+            if t >= 1:
                 centre_and_gain(t - 1)
-            if t < TILES:
-                for h in range(HALVES):
-                    if h == 1 or t >= EARLY_TILES:
-                        form_u(t, h)
-                        state["free"] += 1
-                statistics(t)
-                square(t)
-                if t == TILES - 1:
-                    scale_shift_store(TILES - 2)
-            for m in TSLOT.get(t, ()):
-                for j in range(FILLS):
-                    transpose_tokens(m, j)
-                ready_tiles.append(m)
+            new_halves = range(HALVES) if t >= EARLY_TILES else range(1, HALVES)
+            for h in new_halves:
+                form_u(t, h)
+            statistics(t)
+            if t == LAST:
+                scale_shift_store(LAST - 1)
+            if t < EARLY_TILES:
+                transpose_tokens(t + 4)
+            if t == EARLY_TILES + 1:
+                transpose_tokens(LAST)
             if EARLY_TILES <= t + 2 < TILES:
                 for h in range(HALVES):
                     add_residual_and_bias(t + 2, h)
-            if False and t < TILES:
-                square(t)
-            for m in PSLOT.get(t, ()):
-                arrange_tokens(m)
-            for m in pending:
-                quantise_tokens(m)
-                done_x.append(m)
-            multiply_units()
+            if t == EARLY_TILES:
+                arrange_tokens(LAST)
+            if 1 <= t <= EARLY_TILES:
+                quantise_tokens(t + 3)
+            if t == EARLY_TILES + 2:
+                quantise_tokens(LAST)
+            for _ in new_halves:
+                multiply_next()
+        centre_and_gain(LAST)
+        scale_shift_store(LAST, [half(h) for h in range(HALVES)])

@@ -123,12 +123,12 @@ def tile_disentangledattention_pc_kernel(tc, ff, attn_out, Wf, b_f, ln2_g, ln2_b
             left = slice(0, W_VECTOR_COLS)
             right = slice(W_VECTOR_COLS, BANK)
             nc.scalar.copy(
-                out=w_grouped[g, h][:, right, :].rearrange("p (c i) t -> p c t i", i=4),
-                in_=w_raw[g, h][:, :, right].rearrange("p t (c i) -> p c t i", i=4),
+                out=w_grouped[g, h][:, right, :].rearrange("p (c i) t -> p c t i", i=2),
+                in_=w_raw[g, h][:, :, right].rearrange("p t (c i) -> p c t i", i=2),
             )
             nc.vector.tensor_copy(
-                out=w_grouped[g, h][:, left, :].rearrange("p (c i) t -> p c t i", i=4),
-                in_=w_raw[g, h][:, :, left].rearrange("p t (c i) -> p c t i", i=4),
+                out=w_grouped[g, h][:, left, :].rearrange("p (c i) t -> p c t i", i=2),
+                in_=w_raw[g, h][:, :, left].rearrange("p t (c i) -> p c t i", i=2),
             )
 
         def quantise_weights(g, h):

from contextlib import ExitStack

import concourse.mybir as mybir
from concourse.masks import make_identity

F32 = mybir.dt.float32
BF16 = mybir.dt.bfloat16
U32 = mybir.dt.uint32
U8 = mybir.dt.uint8
FP8X4 = mybir.dt.float8_e4m3fn_x4
ALU = mybir.AluOpType
ACT = mybir.ActivationFunctionType

P = 128
PACK = 4
K_PASS = P * PACK
TOKENS = 1024
K = 3072
N = 1024
EPS = 1e-7
PASSES = K // K_PASS
TILES = TOKENS // P
BANK = 512
HALVES = N // BANK
STEPS = PASSES * HALVES
FILLS = K // 2 // BANK
PASSES_PER_FILL = PASSES // FILLS

EARLY_TILES = 3
ACC_BANKS = EARLY_TILES + 1
STAGE_BANKS = 8 - ACC_BANKS
W_VECTOR_COLS = 304
TOKENS_BEHIND = (-1, 2, 4, STEPS - 2)
TRANSPOSE_STEP = tuple(step + 1 for step in TOKENS_BEHIND)
RESIDUAL_STEP = PASSES
LAST = TILES - 1

FLOPS = 2 * TOKENS * K * N


def tile_disentangledattention_pc_kernel(tc, ff, attn_out, Wf, b_f, ln2_g, ln2_b, out):
    nc = tc.nc
    ff_rows = ff.flatten_outer_dims()
    attn_rows = attn_out.flatten_outer_dims()
    out_rows = out.flatten_outer_dims()

    with ExitStack() as ctx:
        const = ctx.enter_context(tc.tile_pool(name="const", bufs=1))
        ff_pool = ctx.enter_context(tc.tile_pool(name="ff", bufs=TILES))
        attn_pool = ctx.enter_context(tc.tile_pool(name="attn", bufs=TILES))
        w_raw_pool = ctx.enter_context(tc.tile_pool(name="w_raw", bufs=PASSES))
        w_grouped_pool = ctx.enter_context(tc.tile_pool(name="w_grouped", bufs=3))
        arranged_pool = ctx.enter_context(tc.tile_pool(name="arranged", bufs=1))
        x_grouped_pool = ctx.enter_context(tc.tile_pool(name="x_grouped", bufs=2))
        x_pool = ctx.enter_context(tc.tile_pool(name="x", bufs=EARLY_TILES + 3))
        resid_pool = ctx.enter_context(tc.tile_pool(name="resid", bufs=EARLY_TILES * HALVES))
        u_pool = ctx.enter_context(tc.tile_pool(name="u", bufs=EARLY_TILES + 2))
        y_pool = ctx.enter_context(tc.tile_pool(name="y", bufs=3))
        scratch = ctx.enter_context(tc.tile_pool(name="scratch", bufs=2))
        stats = ctx.enter_context(tc.tile_pool(name="stats", bufs=TILES))
        acc_pool = ctx.enter_context(tc.psum_pool(name="acc", bufs=ACC_BANKS))
        stage = ctx.enter_context(tc.psum_pool(name="stage", bufs=STAGE_BANKS))
        ctx.enter_context(tc.manual_schedule())

        def half(h):
            return slice(h * BANK, (h + 1) * BANK)

        ident_words = const.tile([P, P], F32)
        make_identity(nc, ident_words[:])
        ident_bf16 = const.tile([P, P], BF16)
        make_identity(nc, ident_bf16[:])
        eps = const.tile([P, 1], F32)
        nc.vector.memset(eps[:], EPS)
        vector_rows = const.tile([P, N], BF16)
        nc.vector.memset(vector_rows[:].bitcast(U32), 0)
        pick = const.tile([P, 3, P], BF16)
        nc.vector.memset(pick[:].rearrange("p j m -> p (j m)").bitcast(U32), 0)
        for j in range(3):
            nc.vector.memset(pick[32 * j : 32 * j + 1, j, :], 1.0)
        gamma = const.tile([P, N], F32)
        beta = const.tile([P, N], F32)
        warm = const.tile([P, 1], F32)
        nc.scalar.activation(out=warm[:], in_=eps[:], func=ACT.Abs_reciprocal_sqrt)

        w_codes = const.tile([P, PASSES, N], U32, align_bytes=64)
        w_scales = const.tile([P, PASSES, N], U8, align_bytes=64)

        ff_tile, attn_tile, w_raw, w_grouped = {}, {}, {}, {}
        arranged, x_grouped, x_codes, x_scales = {}, {}, {}, {}
        acc, resid, u, y, half_sums, neg_mean, rstd = {}, {}, {}, {}, {}, {}, {}

        def load_tokens(m, pieces=(slice(0, K),)):
            if m not in ff_tile:
                ff_tile[m] = ff_pool.tile([P, K], BF16, name="ff_tile")
            for cols in pieces:
                nc.sync.dma_start(out=ff_tile[m][:, cols], in_=ff_rows[m * P : (m + 1) * P, cols])

        def load_residual(m):
            attn_tile[m] = attn_pool.tile([P, N], BF16, name="attn_tile")
            nc.sync.dma_start(out=attn_tile[m][:], in_=attn_rows[m * P : (m + 1) * P, :])

        def load_weights(g, h):
            w_raw[g, h] = w_raw_pool.tile([P, PACK, BANK], BF16, name="w_raw")
            nc.sync.dma_start(
                out=w_raw[g, h][:],
                in_=Wf[g * K_PASS : (g + 1) * K_PASS, half(h)].rearrange("(p t) c -> p t c", t=PACK),
            )

        def load_vectors():
            for j, vec in enumerate((b_f, ln2_g, ln2_b)):
                nc.sync.dma_start(out=vector_rows[32 * j : 32 * j + 1, :], in_=vec.rearrange("(o n) -> o n", o=1))

        def spread_gain_and_shift(h):
            gamma_bank = stage.tile([P, BANK], F32, name="bank")
            nc.tensor.matmul(out=gamma_bank[:], lhsT=pick[:, 1, :], rhs=vector_rows[:, half(h)], start=True, stop=True)
            nc.vector.tensor_copy(out=gamma[:, half(h)], in_=gamma_bank[:])
            beta_bank = stage.tile([P, BANK], F32, name="bank")
            nc.tensor.matmul(out=beta_bank[:], lhsT=pick[:, 2, :], rhs=vector_rows[:, half(h)], start=True, stop=True)
            nc.scalar.copy(out=beta[:, half(h)], in_=beta_bank[:])

        def regroup_weights(g, h):
            w_grouped[g, h] = w_grouped_pool.tile([P, BANK, PACK], BF16, name="w_grouped", align_bytes=64)
            left = slice(0, W_VECTOR_COLS)
            right = slice(W_VECTOR_COLS, BANK)
            nc.scalar.copy(
                out=w_grouped[g, h][:, right, :].rearrange("p (c i) t -> p c t i", i=2),
                in_=w_raw[g, h][:, :, right].rearrange("p t (c i) -> p c t i", i=2),
            )
            nc.vector.tensor_copy(
                out=w_grouped[g, h][:, left, :].rearrange("p (c i) t -> p c t i", i=2),
                in_=w_raw[g, h][:, :, left].rearrange("p t (c i) -> p c t i", i=2),
            )

        def quantise_weights(g, h):
            nc.vector.quantize_mx(
                out=w_codes[:, g, half(h)].bitcast(FP8X4),
                scales=w_scales[:, g, half(h)],
                in_=w_grouped[g, h][:].rearrange("p c t -> p (c t)"),
            )

        def arrange_tokens(m):
            arranged[m] = arranged_pool.tile([P, K // 2], F32, name="arranged")
            nc.scalar.copy(
                out=arranged[m][:].rearrange("p (g u w) -> p g u w", u=2, w=P),
                in_=ff_tile[m][:].bitcast(F32).rearrange("p (g w u) -> p g u w", u=2, w=P),
            )

        def words_of(m, g, slot):
            if m in arranged:
                first = (2 * g + slot) * P
                return arranged[m][:, first : first + P]
            first = 2 * g * P + slot
            return ff_tile[m][:].bitcast(F32)[:, first : 2 * (g + 1) * P : 2]

        def transpose_tokens(m):
            x_grouped[m] = x_grouped_pool.tile([P, PASSES * P * PACK], BF16, name="x_grouped", align_bytes=64)
            for j in range(FILLS):
                bank = stage.tile([P, BANK], F32, name="bank")
                for q in range(BANK // P):
                    i, slot = divmod(q, 2)
                    words = words_of(m, j * PASSES_PER_FILL + i, slot)
                    nc.tensor.transpose(bank[:, q * P : (q + 1) * P], words, ident_words[:])
                nc.scalar.copy(
                    out=x_grouped[m][:].bitcast(F32)[:, j * BANK : (j + 1) * BANK].rearrange(
                        "p (g r u) -> p g r u", g=PASSES_PER_FILL, u=2
                    ),
                    in_=bank[:].rearrange("p (g u r) -> p g r u", g=PASSES_PER_FILL, u=2),
                )

        def quantise_tokens(m):
            x_codes[m] = x_pool.tile([P, PASSES * P], U32, name="x_codes", align_bytes=64)
            x_scales[m] = x_pool.tile([P, PASSES * P], U8, name="x_scales", align_bytes=64)
            width = PASSES_PER_FILL * P
            for j in range(FILLS):
                nc.vector.quantize_mx(
                    out=x_codes[m][:, j * width : (j + 1) * width].bitcast(FP8X4),
                    scales=x_scales[m][:, j * width : (j + 1) * width],
                    in_=x_grouped[m][:, j * width * PACK : (j + 1) * width * PACK],
                )

        def multiply(m, g, h):
            if g == 0:
                acc[m, h] = acc_pool.tile([P, BANK], F32, name="acc")
            tokens = slice(g * P, (g + 1) * P)
            nc.tensor.matmul_mx(
                out=acc[m, h][:],
                lhsT=x_codes[m][:, tokens].bitcast(FP8X4),
                lhsT_scale=x_scales[m][:, tokens],
                rhs=w_codes[:, g, half(h)].bitcast(FP8X4),
                rhs_scale=w_scales[:, g, half(h)],
                start=(g == 0),
                stop=(g == PASSES - 1),
            )

        def add_residual_and_bias(m, h):
            resid[m, h] = resid_pool.tile([P, BANK], F32, name="resid")
            bank = stage.tile([P, BANK], F32, name="bank")
            nc.tensor.matmul(out=bank[:], lhsT=ident_bf16[:], rhs=attn_tile[m][:, half(h)], start=True, stop=False)
            nc.tensor.matmul(out=bank[:], lhsT=pick[:, 0, :], rhs=vector_rows[:, half(h)], start=False, stop=True)
            nc.scalar.copy(out=resid[m, h][:], in_=bank[:])

        def form_u(m, h):
            if h == 0:
                u[m] = u_pool.tile([P, N], F32, name="u")
                half_sums[m] = stats.tile([P, HALVES], F32, name="half_sums")
            nc.vector.scalar_tensor_tensor(
                out=u[m][:, half(h)],
                in0=acc[m, h][:],
                scalar=1.0,
                in1=resid[m, h][:],
                op0=ALU.mult,
                op1=ALU.add,
                accum_out=half_sums[m][:, h : h + 1],
            )

        def statistics(m):
            neg_mean[m] = stats.tile([P, 1], F32, name="neg_mean")
            scaled = stats.tile([P, HALVES], F32, name="scaled")
            nc.scalar.activation(
                out=scaled[:], in_=half_sums[m][:], func=ACT.Identity, scale=-1.0 / N, accum_out=neg_mean[m][:]
            )
            squares = scratch.tile([P, N], BF16, name="squares")
            sum_squares = stats.tile([P, 1], F32, name="sum_squares")
            nc.scalar.activation(
                out=squares[:], in_=u[m][:], func=ACT.Square, bias=neg_mean[m][:], scale=1.0, accum_out=sum_squares[:]
            )
            rstd[m] = stats.tile([P, 1], F32, name="rstd")
            nc.scalar.activation(
                out=rstd[m][:], in_=sum_squares[:], func=ACT.Abs_reciprocal_sqrt, bias=eps[:], scale=1.0 / N
            )

        def centre_and_gain(m):
            y[m] = y_pool.tile([P, N], F32, name="y")
            nc.vector.scalar_tensor_tensor(
                out=y[m][:], in0=u[m][:], scalar=neg_mean[m][:], in1=gamma[:], op0=ALU.add, op1=ALU.mult
            )

        def scale_shift_store(m, pieces=(slice(0, N),)):
            for cols in pieces:
                nc.vector.scalar_tensor_tensor(
                    out=y[m][:, cols],
                    in0=y[m][:, cols],
                    scalar=rstd[m][:],
                    in1=beta[:, cols],
                    op0=ALU.mult,
                    op1=ALU.add,
                )
                nc.sync.dma_start(out=out_rows[m * P : (m + 1) * P, cols], in_=y[m][:, cols])

        fills = [slice(j * K // FILLS, (j + 1) * K // FILLS) for j in range(FILLS)]
        load_tokens(0, fills[:1])
        load_weights(0, 0)
        load_tokens(0, fills[1:])
        load_vectors()
        for g in range(1, PASSES):
            load_weights(g, 0)
            if g in TOKENS_BEHIND:
                load_tokens(TOKENS_BEHIND.index(g))
        load_residual(0)

        def step_of_product(m, g, h):
            ready = max(PASSES * h + g, TRANSPOSE_STEP[m] + 1) + 1
            return max(ready, RESIDUAL_STEP + m + 1) if h else ready

        early_products = [(m, g, h) for h in range(HALVES) for m in range(EARLY_TILES) for g in range(PASSES)]
        for step in range(STEPS + 1):
            h, g = divmod(step, PASSES)
            if 1 <= step <= PASSES:
                load_weights(step - 1, 1)
                if step < EARLY_TILES:
                    load_residual(step)
                if step - 1 + PASSES in TOKENS_BEHIND:
                    load_tokens(TOKENS_BEHIND.index(step - 1 + PASSES))
            if step == PASSES:
                for m in range(EARLY_TILES + 1, TILES):
                    load_tokens(m)
                    load_residual(m - 1)
                load_residual(LAST)
            if step < STEPS:
                regroup_weights(g, h)
            if 1 <= step <= HALVES:
                spread_gain_and_shift(step - 1)
            if step - 1 in TRANSPOSE_STEP:
                quantise_tokens(TRANSPOSE_STEP.index(step - 1))
            if 0 <= step - 1 - RESIDUAL_STEP < EARLY_TILES:
                form_u(step - 1 - RESIDUAL_STEP, 0)
            if step < STEPS:
                quantise_weights(g, h)
            if step in TRANSPOSE_STEP:
                transpose_tokens(TRANSPOSE_STEP.index(step))
            if 0 <= step - RESIDUAL_STEP < EARLY_TILES:
                add_residual_and_bias(step - RESIDUAL_STEP, 0)
            if step == RESIDUAL_STEP + EARLY_TILES:
                for m in range(EARLY_TILES):
                    add_residual_and_bias(m, 1)
            for m, gg, hh in early_products:
                if step_of_product(m, gg, hh) == step:
                    multiply(m, gg, hh)

        later_products = [(m, h) for m in range(EARLY_TILES, TILES) for h in range(HALVES)]

        def multiply_next():
            if later_products:
                m, h = later_products.pop(0)
                for g in range(PASSES):
                    multiply(m, g, h)

        multiply_next()
        for t in range(TILES):
            if t >= 2:
                scale_shift_store(t - 2)
            if t >= 1:
                centre_and_gain(t - 1)
            new_halves = range(HALVES) if t >= EARLY_TILES else range(1, HALVES)
            for h in new_halves:
                form_u(t, h)
            statistics(t)
            if t == LAST:
                scale_shift_store(LAST - 1)
            if t < EARLY_TILES:
                transpose_tokens(t + 4)
            if t == EARLY_TILES + 1:
                transpose_tokens(LAST)
            if EARLY_TILES <= t + 2 < TILES:
                for h in range(HALVES):
                    add_residual_and_bias(t + 2, h)
            if t == EARLY_TILES:
                arrange_tokens(LAST)
            if 1 <= t <= EARLY_TILES:
                quantise_tokens(t + 3)
            if t == EARLY_TILES + 2:
                quantise_tokens(LAST)
            for _ in new_halves:
                multiply_next()
        centre_and_gain(LAST)
        scale_shift_store(LAST, [half(h) for h in range(HALVES)])
